import numpy as np
import ml_dtypes


def mxq(x, axis, fmt="e4m3"):
    dtype, down = {"e4m3": (ml_dtypes.float8_e4m3fn, 7), "e5m2": (ml_dtypes.float8_e5m2, 14)}[fmt]
    v = np.moveaxis(np.asarray(x, np.float32).astype(ml_dtypes.bfloat16).astype(np.float64), axis, -1)
    blocks = v.reshape(v.shape[:-1] + (-1, 32))
    amax = np.abs(blocks).max(-1, keepdims=True)
    byte = np.maximum(np.where(amax > 0, np.frexp(amax)[1] - 1 + 127, 0) - down, 1)
    scale = np.exp2(byte - 127.0)
    codes = (blocks / scale).astype(np.float32).astype(dtype).astype(np.float64)
    return np.moveaxis((codes * scale).reshape(v.shape), -1, axis)


WIDE = False


def mx_kscale(k):
    if not WIDE:
        return np.ones(k)
    levels = np.array([10, -10, 5, -5, 0])
    if k % 512:
        return np.exp2(np.random.permutation(np.resize(levels, k // 32))).repeat(32)
    a = np.empty((k // 512, 16))
    for p in range(k // 512):
        a[p, :8] = np.random.permutation(np.resize(levels, 8))
        for g in range(8):
            far = levels[np.abs(levels - a[p, g]) >= 10]
            a[p, g + 8] = far[np.random.randint(len(far))]
    return np.exp2(a.ravel()).repeat(32)


BF16 = ml_dtypes.bfloat16


def bf(x):
    return np.asarray(x, np.float32).astype(BF16)


def f64(x):
    return np.asarray(x).astype(np.float64)


N, NFEAT, NHEADS, NHID, NCLASS = 1024, 512, 4, 128, 128
P = 0.08


def elu(v):
    return np.where(v > 0, v, np.exp(np.minimum(v, 0.0)) - 1.0)


def setup_inputs():
    s, t = mx_kscale(NFEAT), mx_kscale(N)
    edges = np.random.random((N, N)) < P
    return {"x": bf(np.random.standard_normal((N, NFEAT)) * s / t[:, None]),
            "adj": bf(edges * (0.5 + np.random.random((N, N))) * t),
            "W0": bf(np.random.standard_normal((NHEADS, NFEAT, NHID)) * 1.5 / np.sqrt(NFEAT * P * N) / s[:, None])}


def reference(x, adj, W0):
    h = f64(bf(mxq(f64(x), 1, "e4m3") @ mxq(f64(W0), 1, "e4m3")))
    hp = mxq(f64(adj), 1, "e4m3") @ mxq(h, 1, "e4m3")
    return elu(hp).transpose(1, 0, 2).reshape(N, NHEADS * NHID)

@@ -1,0 +1,226 @@
+from contextlib import ExitStack
+
+import concourse.mybir as mybir
+from concourse.masks import make_identity
+
+FLOPS = 2 * 1024 * 512 * 512 + 2 * 1024 * 1024 * 512
+
+F32 = mybir.dt.float32
+BF16 = mybir.dt.bfloat16
+U32 = mybir.dt.uint32
+U8 = mybir.dt.uint8
+FP8X4 = mybir.dt.float8_e4m3fn_x4
+ALU = mybir.AluOpType
+ACTF = mybir.ActivationFunctionType
+
+P = 128
+G_BANK_DT = BF16
+TP_BANKS = 3
+ACC_BANKS = 5
+
+
+def tile_gat_pa_kernel(tc, x, adj, W0, out):
+    nc = tc.nc
+    with ExitStack() as ctx:
+        sb = ctx.enter_context(tc.tile_pool(name="sb", bufs=1))
+        ps = ctx.enter_context(tc.psum_pool(name="ps", bufs=1))
+        ctx.enter_context(tc.manual_schedule())
+
+        x_raw, x_tp, x_grp, x_cod, x_scl = {}, {}, {}, {}, {}
+        w_raw, w_grp, w_cod, w_scl = {}, {}, {}, {}
+        a_raw, a_tp, a_grp, a_cod, a_scl = {}, {}, {}, {}, {}
+        g_ps, g_grp, g_cod, g_scl = {}, {}, {}, {}
+        p_ps, e_sb, q_sb = {}, {}, {}
+
+        def load_x(g, b):
+            x_raw[g, b] = sb.tile([P, 2, 512], BF16, name="x_raw%d%d" % (g, b))
+            rows = x[512 * g:512 * (g + 1), :].rearrange("(m t) k -> m t k", t=4)
+            nc.sync.dma_start(out=x_raw[g, b][:], in_=rows[:, 2 * b:2 * b + 2, :])
+
+        def load_w(a):
+            w_raw[a] = sb.tile([P, 2, 4, P], BF16, name="w_raw%d" % a)
+            nc.sync.dma_start(out=w_raw[a][:], in_=W0[2 * a:2 * a + 2].rearrange("h (p j) c -> p h j c", j=4))
+
+        def load_adj(i):
+            a_raw[i] = sb.tile([P, 1024], BF16, name="a_raw%d" % i)
+            nc.sync.dma_start(out=a_raw[i][:], in_=adj[P * i:P * (i + 1), :])
+
+        load_x(0, 0)
+        load_x(0, 1)
+        load_x(1, 0)
+        load_w(0)
+        load_x(1, 1)
+        load_w(1)
+        for i in range(8):
+            load_adj(i)
+
+        zeros = sb.tile([P, 512], BF16, name="zeros")
+        nc.vector.memset(zeros[:], 0.0)
+        idle_ps = ps.tile([P, 512], F32, name="idle_ps", tag="acc", bufs=ACC_BANKS)
+        exp_in = sb.tile([P, 1], F32, name="exp_in")
+        exp_out = sb.tile([P, 1], F32, name="exp_out")
+        nc.vector.memset(exp_in[:], 0.0)
+        nc.scalar.activation(out=exp_out[:], in_=exp_in[:], func=ACTF.Exp)
+        ident = sb.tile([P, P], F32, name="ident")
+        make_identity(nc, ident[:])
+
+        def keep_clock(n):
+            for r in range(n):
+                nc.tensor.matmul(out=idle_ps[:], lhsT=zeros[:, 0:P], rhs=zeros[:], start=True, stop=True)
+
+        def transpose_words(name, raw2d):
+            bank = ps.tile([P, 4, P], F32, name=name, tag="tp", bufs=TP_BANKS)
+            words = raw2d.bitcast(F32)
+            for s in range(2):
+                for u in range(2):
+                    nc.tensor.transpose(bank[:, 2 * s + u, :], words[:, 256 * s + u:256 * (s + 1):2], ident[:])
+            return bank
+
+        def group_words(name, bank):
+            grp = sb.tile([P, 2, P, 4], BF16, name=name, align_bytes=64)
+            nc.scalar.copy(out=grp[:].bitcast(F32), in_=bank[:].rearrange("p (s u) r -> p s r u", u=2))
+            return grp
+
+        def quantize(name, grp2d, width):
+            cod = sb.tile([P, width], U32, name=name + "_cod", align_bytes=64)
+            scl = sb.tile([P, width], U8, name=name + "_scl", align_bytes=64)
+            nc.vector.quantize_mx(out=cod[:].bitcast(FP8X4), scales=scl[:], in_=grp2d)
+            return cod, scl
+
+        def tx(g, b):
+            x_tp[g, b] = transpose_words("x_tp%d%d" % (g, b), x_raw[g, b][:].rearrange("p t k -> p (t k)"))
+
+        def cx(g, b):
+            x_grp[g, b] = group_words("x_grp%d%d" % (g, b), x_tp[g, b])
+
+        def qx(g, b):
+            x_cod[g, b], x_scl[g, b] = quantize("x%d%d" % (g, b), x_grp[g, b][:].rearrange("p s m j -> p (s m j)"), 256)
+
+        def wi(h):
+            w_grp[h] = sb.tile([P, P, 4], BF16, name="w_grp%d" % h, align_bytes=64)
+            nc.vector.tensor_copy(out=w_grp[h][:], in_=w_raw[h // 2][:, h % 2].rearrange("p j c -> p c j"))
+
+        def qw(h):
+            w_cod[h], w_scl[h] = quantize("w%d" % h, w_grp[h][:].rearrange("p c j -> p (c j)"), P)
+
+        def ta(i):
+            a_tp[i] = transpose_words("a_tp%d" % i, a_raw[i][:])
+
+        def ca(i):
+            a_grp[i] = group_words("a_grp%d" % i, a_tp[i])
+
+        def qa(i):
+            a_cod[i], a_scl[i] = quantize("a%d" % i, a_grp[i][:].rearrange("p g r j -> p (g r j)"), 256)
+
+        for g in range(2):
+            g_cod[g] = sb.tile([P, 512], U32, name="g_cod%d" % g, align_bytes=64)
+            g_scl[g] = sb.tile([P, 512], U8, name="g_scl%d" % g, align_bytes=64)
+
+        def s1(g, h):
+            g_ps[g, h] = ps.tile([P, 4, P], G_BANK_DT, name="g_ps%d%d" % (g, h), tag="acc", bufs=ACC_BANKS)
+            for t in range(4):
+                cols = slice(P * (t % 2), P * (t % 2 + 1))
+                nc.tensor.matmul_mx(out=g_ps[g, h][:, t, :],
+                                    lhsT=x_cod[g, t // 2][:, cols].bitcast(FP8X4), lhsT_scale=x_scl[g, t // 2][:, cols],
+                                    rhs=w_cod[h][:].bitcast(FP8X4), rhs_scale=w_scl[h][:],
+                                    start=True, stop=True)
+
+        def cg(g, h):
+            g_grp[g, h] = sb.tile([P, P, 4], BF16, name="g_grp%d%d" % (g, h), align_bytes=64)
+            if h < 3:
+                nc.scalar.copy(out=g_grp[g, h][:], in_=g_ps[g, h][:].rearrange("p t c -> p c t"))
+            else:
+                nc.vector.tensor_copy(out=g_grp[g, h][:], in_=g_ps[g, h][:].rearrange("p t c -> p c t"))
+
+        def qg(g, h):
+            cols = slice(P * h, P * (h + 1))
+            nc.vector.quantize_mx(out=g_cod[g][:, cols].bitcast(FP8X4), scales=g_scl[g][:, cols],
+                                  in_=g_grp[g, h][:].rearrange("p c t -> p (c t)"))
+
+        def s2(i):
+            p_ps[i] = ps.tile([P, 512], F32, name="p_ps%d" % i, tag="acc", bufs=ACC_BANKS)
+            for g in range(2):
+                cols = slice(P * g, P * (g + 1))
+                nc.tensor.matmul_mx(out=p_ps[i][:],
+                                    lhsT=a_cod[i][:, cols].bitcast(FP8X4), lhsT_scale=a_scl[i][:, cols],
+                                    rhs=g_cod[g][:].bitcast(FP8X4), rhs_scale=g_scl[g][:],
+                                    start=(g == 0), stop=(g == 1))
+
+        def ee(i):
+            e_sb[i] = sb.tile([P, 512], F32, name="e_sb%d" % i)
+            nc.scalar.activation(out=e_sb[i][:], in_=p_ps[i][:], func=ACTF.Exp)
+
+        def mm(i):
+            q_sb[i] = sb.tile([P, 512], F32, name="q_sb%d" % i)
+            if i < 6:
+                nc.vector.tensor_scalar(out=q_sb[i][:], in0=e_sb[i][:], scalar1=-1.0, scalar2=0.0,
+                                        op0=ALU.add, op1=ALU.min)
+            else:
+                nc.scalar.activation(out=q_sb[i][:], in_=e_sb[i][:], func=ACTF.Relu, scale=-1.0, bias=1.0)
+
+        def ff(i):
+            o_sb = sb.tile([P, 512], F32, name="o_sb%d" % i)
+            nc.vector.scalar_tensor_tensor(out=o_sb[:], in0=p_ps[i][:], scalar=0.0, in1=q_sb[i][:],
+                                           op0=ALU.max, op1=(ALU.add if i < 6 else ALU.subtract))
+            nc.sync.dma_start(out=out[P * i:P * (i + 1), :], in_=o_sb[:])
+
+        keep_clock(4)
+        tx(0, 0)
+        tx(0, 1)
+        keep_clock(2)
+        tx(1, 0)
+        cx(0, 0)
+        tx(1, 1)
+        cx(0, 1)
+        cx(1, 0)
+        cx(1, 1)
+        qx(0, 0)
+        wi(0)
+        qx(0, 1)
+        wi(1)
+        qw(0)
+        qw(1)
+        wi(2)
+        qx(1, 0)
+        wi(3)
+        qw(2)
+        qx(1, 1)
+        qw(3)
+
+        for g in range(2):
+            s1(g, 0)
+            s1(g, 1)
+            ta(g)
+            s1(g, 2)
+            s1(g, 3)
+            cg(g, 0)
+            cg(g, 1)
+            cg(g, 2)
+            ca(g)
+            qg(g, 0)
+            qg(g, 1)
+            cg(g, 3)
+            qg(g, 2)
+            qg(g, 3)
+            qa(g)
+
+        for j in range(4):
+            now = [2 * j, 2 * j + 1]
+            ahead = [2 * j + 2, 2 * j + 3] if j < 3 else []
+            for i in ahead:
+                ta(i)
+            for i in now:
+                s2(i)
+            for i in ahead:
+                ca(i)
+            for i in now:
+                ee(i)
+            for k in range(2):
+                if j > 0:
+                    ff(2 * j - 2 + k)
+                if j < 3:
+                    qa(2 * j + 2 + k)
+            for i in now:
+                mm(i)
+        ff(6)
+        ff(7)

@@ -32,24 +32,27 @@ def tile_gat_pa_kernel(tc, x, adj, W0, out):
         g_ps, g_grp, g_cod, g_scl = {}, {}, {}, {}
         p_ps, e_sb, q_sb = {}, {}, {}
 
-        def load_x(g, b):
-            x_raw[g, b] = sb.tile([P, 2, 512], BF16, name="x_raw%d%d" % (g, b))
+        def load_x(g, t0, n):
+            raw = sb.tile([P, n, 512], BF16, name="x_raw%d%d" % (g, t0))
             rows = x[512 * g:512 * (g + 1), :].rearrange("(m t) k -> m t k", t=4)
-            nc.sync.dma_start(out=x_raw[g, b][:], in_=rows[:, 2 * b:2 * b + 2, :])
+            nc.sync.dma_start(out=raw[:], in_=rows[:, t0:t0 + n, :])
+            for s in range(n):
+                x_raw[g, t0 + s] = raw[:, s, :]
 
         def load_w(a):
             w_raw[a] = sb.tile([P, 2, 4, P], BF16, name="w_raw%d" % a)
             nc.sync.dma_start(out=w_raw[a][:], in_=W0[2 * a:2 * a + 2].rearrange("h (p j) c -> p h j c", j=4))
 
         def load_adj(i):
-            a_raw[i] = sb.tile([P, 1024], BF16, name="a_raw%d" % i)
-            nc.sync.dma_start(out=a_raw[i][:], in_=adj[P * i:P * (i + 1), :])
+            a_raw[i] = sb.tile([P, 2, 512], BF16, name="a_raw%d" % i)
+            nc.sync.dma_start(out=a_raw[i][:], in_=adj[P * i:P * (i + 1), :].rearrange("n (g m) -> n g m", g=2))
 
-        load_x(0, 0)
-        load_x(0, 1)
-        load_x(1, 0)
+        load_x(0, 0, 2)
+        load_x(0, 2, 2)
+        load_x(1, 0, 2)
         load_w(0)
-        load_x(1, 1)
+        load_x(1, 2, 1)
+        load_x(1, 3, 1)
         load_w(1)
         for i in range(8):
             load_adj(i)
@@ -68,17 +71,18 @@ def tile_gat_pa_kernel(tc, x, adj, W0, out):
             for r in range(n):
                 nc.tensor.matmul(out=idle_ps[:], lhsT=zeros[:, 0:P], rhs=zeros[:], start=True, stop=True)
 
-        def transpose_words(name, raw2d):
+        def transpose_words(name, rows512):
             bank = ps.tile([P, 4, P], F32, name=name, tag="tp", bufs=TP_BANKS)
-            words = raw2d.bitcast(F32)
             for s in range(2):
+                words = rows512[s].bitcast(F32)
                 for u in range(2):
-                    nc.tensor.transpose(bank[:, 2 * s + u, :], words[:, 256 * s + u:256 * (s + 1):2], ident[:])
+                    nc.tensor.transpose(bank[:, 2 * s + u, :], words[:, u:256:2], ident[:])
             return bank
 
-        def group_words(name, bank):
+        def group_words(name, bank, on_vector=False):
             grp = sb.tile([P, 2, P, 4], BF16, name=name, align_bytes=64)
-            nc.scalar.copy(out=grp[:].bitcast(F32), in_=bank[:].rearrange("p (s u) r -> p s r u", u=2))
+            copy = nc.vector.tensor_copy if on_vector else nc.scalar.copy
+            copy(out=grp[:].bitcast(F32), in_=bank[:].rearrange("p (s u) r -> p s r u", u=2))
             return grp
 
         def quantize(name, grp2d, width):
@@ -88,7 +92,7 @@ def tile_gat_pa_kernel(tc, x, adj, W0, out):
             return cod, scl
 
         def tx(g, b):
-            x_tp[g, b] = transpose_words("x_tp%d%d" % (g, b), x_raw[g, b][:].rearrange("p t k -> p (t k)"))
+            x_tp[g, b] = transpose_words("x_tp%d%d" % (g, b), [x_raw[g, 2 * b], x_raw[g, 2 * b + 1]])
 
         def cx(g, b):
             x_grp[g, b] = group_words("x_grp%d%d" % (g, b), x_tp[g, b])
@@ -98,16 +102,17 @@ def tile_gat_pa_kernel(tc, x, adj, W0, out):
 
         def wi(h):
             w_grp[h] = sb.tile([P, P, 4], BF16, name="w_grp%d" % h, align_bytes=64)
-            nc.vector.tensor_copy(out=w_grp[h][:], in_=w_raw[h // 2][:, h % 2].rearrange("p j c -> p c j"))
+            copy = nc.scalar.copy if h == 1 else nc.vector.tensor_copy
+            copy(out=w_grp[h][:], in_=w_raw[h // 2][:, h % 2].rearrange("p j c -> p c j"))
 
         def qw(h):
             w_cod[h], w_scl[h] = quantize("w%d" % h, w_grp[h][:].rearrange("p c j -> p (c j)"), P)
 
         def ta(i):
-            a_tp[i] = transpose_words("a_tp%d" % i, a_raw[i][:])
+            a_tp[i] = transpose_words("a_tp%d" % i, [a_raw[i][:, 0, :], a_raw[i][:, 1, :]])
 
         def ca(i):
-            a_grp[i] = group_words("a_grp%d" % i, a_tp[i])
+            a_grp[i] = group_words("a_grp%d" % i, a_tp[i], on_vector=(i == 0))
 
         def qa(i):
             a_cod[i], a_scl[i] = quantize("a%d" % i, a_grp[i][:].rearrange("p g r j -> p (g r j)"), 256)
@@ -127,42 +132,43 @@ def tile_gat_pa_kernel(tc, x, adj, W0, out):
 
         def cg(g, h):
             g_grp[g, h] = sb.tile([P, P, 4], BF16, name="g_grp%d%d" % (g, h), align_bytes=64)
-            if h < 3:
-                nc.scalar.copy(out=g_grp[g, h][:], in_=g_ps[g, h][:].rearrange("p t c -> p c t"))
-            else:
-                nc.vector.tensor_copy(out=g_grp[g, h][:], in_=g_ps[g, h][:].rearrange("p t c -> p c t"))
+            copy = nc.scalar.copy if h < 3 else nc.vector.tensor_copy
+            copy(out=g_grp[g, h][:], in_=g_ps[g, h][:].rearrange("p t c -> p c t"))
 
         def qg(g, h):
             cols = slice(P * h, P * (h + 1))
             nc.vector.quantize_mx(out=g_cod[g][:, cols].bitcast(FP8X4), scales=g_scl[g][:, cols],
                                   in_=g_grp[g, h][:].rearrange("p c t -> p (c t)"))
 
-        def s2(i):
-            p_ps[i] = ps.tile([P, 512], F32, name="p_ps%d" % i, tag="acc", bufs=ACC_BANKS)
+        def s2(piece):
+            i, c0, width = piece
+            p_ps[piece] = ps.tile([P, width], F32, name="p_ps%d_%d" % (i, c0), tag="acc", bufs=ACC_BANKS)
             for g in range(2):
-                cols = slice(P * g, P * (g + 1))
-                nc.tensor.matmul_mx(out=p_ps[i][:],
-                                    lhsT=a_cod[i][:, cols].bitcast(FP8X4), lhsT_scale=a_scl[i][:, cols],
-                                    rhs=g_cod[g][:].bitcast(FP8X4), rhs_scale=g_scl[g][:],
+                rows = slice(P * g, P * (g + 1))
+                cols = slice(c0, c0 + width)
+                nc.tensor.matmul_mx(out=p_ps[piece][:],
+                                    lhsT=a_cod[i][:, rows].bitcast(FP8X4), lhsT_scale=a_scl[i][:, rows],
+                                    rhs=g_cod[g][:, cols].bitcast(FP8X4), rhs_scale=g_scl[g][:, cols],
                                     start=(g == 0), stop=(g == 1))
 
-        def ee(i):
-            e_sb[i] = sb.tile([P, 512], F32, name="e_sb%d" % i)
-            nc.scalar.activation(out=e_sb[i][:], in_=p_ps[i][:], func=ACTF.Exp)
+        def ee(piece):
+            e_sb[piece] = sb.tile([P, piece[2]], F32, name="e_sb%d_%d" % piece[0:2])
+            nc.scalar.activation(out=e_sb[piece][:], in_=p_ps[piece][:], func=ACTF.Exp)
 
-        def mm(i):
-            q_sb[i] = sb.tile([P, 512], F32, name="q_sb%d" % i)
-            if i < 6:
-                nc.vector.tensor_scalar(out=q_sb[i][:], in0=e_sb[i][:], scalar1=-1.0, scalar2=0.0,
-                                        op0=ALU.add, op1=ALU.min)
+        def mm(piece):
+            q_sb[piece] = sb.tile([P, piece[2]], F32, name="q_sb%d_%d" % piece[0:2])
+            if piece[0] == 6:
+                nc.scalar.activation(out=q_sb[piece][:], in_=e_sb[piece][:], func=ACTF.Relu, scale=-1.0, bias=1.0)
             else:
-                nc.scalar.activation(out=q_sb[i][:], in_=e_sb[i][:], func=ACTF.Relu, scale=-1.0, bias=1.0)
+                nc.vector.tensor_scalar(out=q_sb[piece][:], in0=e_sb[piece][:], scalar1=-1.0, scalar2=0.0,
+                                        op0=ALU.add, op1=ALU.min)
 
-        def ff(i):
-            o_sb = sb.tile([P, 512], F32, name="o_sb%d" % i)
-            nc.vector.scalar_tensor_tensor(out=o_sb[:], in0=p_ps[i][:], scalar=0.0, in1=q_sb[i][:],
-                                           op0=ALU.max, op1=(ALU.add if i < 6 else ALU.subtract))
-            nc.sync.dma_start(out=out[P * i:P * (i + 1), :], in_=o_sb[:])
+        def ff(piece):
+            i, c0, width = piece
+            o_sb = sb.tile([P, width], F32, name="o_sb%d_%d" % (i, c0))
+            nc.vector.scalar_tensor_tensor(out=o_sb[:], in0=p_ps[piece][:], scalar=0.0, in1=q_sb[piece][:],
+                                           op0=ALU.max, op1=(ALU.subtract if i == 6 else ALU.add))
+            nc.sync.dma_start(out=out[P * i:P * (i + 1), c0:c0 + width], in_=o_sb[:])
 
         keep_clock(4)
         tx(0, 0)
@@ -172,20 +178,20 @@ def tile_gat_pa_kernel(tc, x, adj, W0, out):
         cx(0, 0)
         tx(1, 1)
         cx(0, 1)
+        wi(1)
         cx(1, 0)
         cx(1, 1)
         qx(0, 0)
         wi(0)
         qx(0, 1)
-        wi(1)
         qw(0)
         qw(1)
         wi(2)
-        qx(1, 0)
         wi(3)
         qw(2)
-        qx(1, 1)
         qw(3)
+        qx(1, 0)
+        qx(1, 1)
 
         for g in range(2):
             s1(g, 0)
@@ -193,10 +199,13 @@ def tile_gat_pa_kernel(tc, x, adj, W0, out):
             ta(g)
             s1(g, 2)
             s1(g, 3)
+            if g == 0:
+                ca(0)
             cg(g, 0)
             cg(g, 1)
             cg(g, 2)
-            ca(g)
+            if g == 1:
+                ca(1)
             qg(g, 0)
             qg(g, 1)
             cg(g, 3)
@@ -204,23 +213,36 @@ def tile_gat_pa_kernel(tc, x, adj, W0, out):
             qg(g, 3)
             qa(g)
 
-        for j in range(4):
-            now = [2 * j, 2 * j + 1]
-            ahead = [2 * j + 2, 2 * j + 3] if j < 3 else []
+        whole = [(i, 0, 512) for i in range(7)]
+        halves = [(7, 0, 256), (7, 256, 256)]
+        for j in range(3):
+            now = whole[2 * j:2 * j + 2]
+            ahead = [2 * j + 2, 2 * j + 3]
             for i in ahead:
                 ta(i)
-            for i in now:
-                s2(i)
+            for piece in now:
+                s2(piece)
             for i in ahead:
                 ca(i)
-            for i in now:
-                ee(i)
-            for k in range(2):
-                if j > 0:
-                    ff(2 * j - 2 + k)
-                if j < 3:
-                    qa(2 * j + 2 + k)
-            for i in now:
-                mm(i)
-        ff(6)
-        ff(7)
+            for piece in now:
+                ee(piece)
+            if j > 0:
+                ff(whole[2 * j - 2])
+            for i in ahead:
+                qa(i)
+            if j > 0:
+                ff(whole[2 * j - 1])
+            for piece in now:
+                mm(piece)
+        for piece in [whole[6]] + halves:
+            s2(piece)
+        ee(whole[6])
+        mm(whole[6])
+        for piece in halves:
+            ee(piece)
+        for piece in whole[4:7]:
+            ff(piece)
+        for piece in halves:
+            mm(piece)
+        for piece in halves:
+            ff(piece)

@@ -14,9 +14,73 @@ ALU = mybir.AluOpType
 ACTF = mybir.ActivationFunctionType
 
 P = 128
-G_BANK_DT = BF16
-TP_BANKS = 3
-ACC_BANKS = 5
+BANKS = {"tp": 3, "acc": 5}
+READERS = {"tx": 1, "ta": 1, "s1": 1, "s2": 2}
+SORTED_FIRST = (4, 5, 6, 7)
+
+
+def queues():
+    whole = [(i, 0, 512) for i in range(7)]
+    halves = [(7, 0, 256), (7, 256, 256)]
+    pieces = whole + halves
+    on_gpsimd = ()
+    on_scalar = (6,)
+
+    def each(op, strips):
+        return [((op,) + p, None) for p in pieces if p[0] in strips]
+
+    def plain(op, args):
+        return [((op,) + tuple(a), None) for a in args]
+
+    def opens(op, args, tag):
+        return [((op,) + tuple(a), tag) for a in args]
+
+    pe = [(("d", 4, 0), "acc")] + opens("tx", [(0, 0), (0, 1)], "tp") + [(("d", 2, 1), None)] + opens("tx", [(1, 0), (1, 1)], "tp")
+    s = plain("cx", [(0, 0), (0, 1)]) + plain("wi", [(1,)]) + plain("cx", [(1, 0), (1, 1)])
+    v = plain("qx", [(0, 0)]) + plain("wi", [(0,)]) + plain("qx", [(0, 1)]) + plain("qw", [(0,), (1,)])
+    v += plain("wi", [(2,), (3,)]) + plain("qw", [(2,), (3,)]) + plain("qx", [(1, 0), (1, 1)])
+    g = []
+    for h in range(2):
+        pe += opens("s1", [(h, 0), (h, 1)], "acc") + opens("ta", [(h,)], "tp") + opens("s1", [(h, 2), (h, 3)], "acc")
+        s += plain("cg", [(h, 0), (h, 1), (h, 2)])
+        if h == 0:
+            v += plain("ca", [(0,)])
+        else:
+            s += plain("ca", [(1,)])
+        v += plain("qg", [(h, 0), (h, 1)]) + plain("cg", [(h, 3)]) + plain("qg", [(h, 2), (h, 3)]) + plain("qa", [(h,)])
+
+    def affine(strips):
+        for i in strips:
+            if i in on_gpsimd:
+                g.extend(each("mm", (i,)))
+            elif i in on_scalar:
+                s.extend(each("mm", (i,)))
+            else:
+                v.extend(each("mm", (i,)))
+
+    for j in range(3):
+        now = (2 * j, 2 * j + 1)
+        ahead = [(2 * j + 2,), (2 * j + 3,)]
+        pe += opens("ta", ahead, "tp") + opens("s2", [p for p in pieces if p[0] in now], "acc")
+        s += plain("ca", ahead) + each("ee", now)
+        if j > 0:
+            v += each("ff", (2 * j - 2,))
+        if j == 0:
+            v += plain("di", [(4,), (5,)])
+        v += plain("qa", ahead)
+        if j == 0:
+            v += plain("di", [(6,), (7,)])
+        if j > 0:
+            v += each("ff", (2 * j - 1,))
+        affine(now)
+    pe += opens("s2", [p for p in pieces if p[0] in (6, 7)], "acc")
+    s += each("ee", (6,))
+    affine((6,))
+    s += each("ee", (7,))
+    v += each("ff", (4, 5, 6))
+    affine((7,))
+    v += each("ff", (7,))
+    return {"PE": pe, "S": s, "V": v, "G": g}
 
 
 def tile_gat_pa_kernel(tc, x, adj, W0, out):
@@ -29,8 +93,10 @@ def tile_gat_pa_kernel(tc, x, adj, W0, out):
         x_raw, x_tp, x_grp, x_cod, x_scl = {}, {}, {}, {}, {}
         w_raw, w_grp, w_cod, w_scl = {}, {}, {}, {}
         a_raw, a_tp, a_grp, a_cod, a_scl = {}, {}, {}, {}, {}
+        a_srt = {}
         g_ps, g_grp, g_cod, g_scl = {}, {}, {}, {}
         p_ps, e_sb, q_sb = {}, {}, {}
+        idle = {}
 
         def load_x(g, t0, n):
             raw = sb.tile([P, n, 512], BF16, name="x_raw%d%d" % (g, t0))
@@ -59,30 +125,33 @@ def tile_gat_pa_kernel(tc, x, adj, W0, out):
 
         zeros = sb.tile([P, 512], BF16, name="zeros")
         nc.vector.memset(zeros[:], 0.0)
-        idle_ps = ps.tile([P, 512], F32, name="idle_ps", tag="acc", bufs=ACC_BANKS)
         exp_in = sb.tile([P, 1], F32, name="exp_in")
         exp_out = sb.tile([P, 1], F32, name="exp_out")
         nc.vector.memset(exp_in[:], 0.0)
         nc.scalar.activation(out=exp_out[:], in_=exp_in[:], func=ACTF.Exp)
         ident = sb.tile([P, P], F32, name="ident")
         make_identity(nc, ident[:])
+        for g in range(2):
+            g_cod[g] = sb.tile([P, 512], U32, name="g_cod%d" % g, align_bytes=64)
+            g_scl[g] = sb.tile([P, 512], U8, name="g_scl%d" % g, align_bytes=64)
 
-        def keep_clock(n):
-            for r in range(n):
-                nc.tensor.matmul(out=idle_ps[:], lhsT=zeros[:, 0:P], rhs=zeros[:], start=True, stop=True)
+        def copier(eng):
+            return nc.vector.tensor_copy if eng == "V" else nc.scalar.copy
 
-        def transpose_words(name, rows512):
-            bank = ps.tile([P, 4, P], F32, name=name, tag="tp", bufs=TP_BANKS)
+        def bank(shape, dt, name, tag):
+            return ps.tile(shape, dt, name=name, tag=tag, bufs=BANKS[tag])
+
+        def transpose_words(name, rows512, tag):
+            t = bank([P, 4, P], F32, name, tag)
             for s in range(2):
                 words = rows512[s].bitcast(F32)
                 for u in range(2):
-                    nc.tensor.transpose(bank[:, 2 * s + u, :], words[:, u:256:2], ident[:])
-            return bank
+                    nc.tensor.transpose(t[:, 2 * s + u, :], words[:, u:256:2], ident[:])
+            return t
 
-        def group_words(name, bank, on_vector=False):
+        def group_words(eng, name, t):
             grp = sb.tile([P, 2, P, 4], BF16, name=name, align_bytes=64)
-            copy = nc.vector.tensor_copy if on_vector else nc.scalar.copy
-            copy(out=grp[:].bitcast(F32), in_=bank[:].rearrange("p (s u) r -> p s r u", u=2))
+            copier(eng)(out=grp[:].bitcast(F32), in_=t[:].rearrange("p (s u) r -> p s r u", u=2))
             return grp
 
         def quantize(name, grp2d, width):
@@ -91,38 +160,53 @@ def tile_gat_pa_kernel(tc, x, adj, W0, out):
             nc.vector.quantize_mx(out=cod[:].bitcast(FP8X4), scales=scl[:], in_=grp2d)
             return cod, scl
 
-        def tx(g, b):
-            x_tp[g, b] = transpose_words("x_tp%d%d" % (g, b), [x_raw[g, 2 * b], x_raw[g, 2 * b + 1]])
+        def op_d(eng, tag, n, k):
+            if tag is not None:
+                idle["ps"] = bank([P, 512], F32, "idle_ps", tag)
+            for r in range(n):
+                nc.tensor.matmul(out=idle["ps"][:], lhsT=zeros[:, 0:P], rhs=zeros[:], start=True, stop=True)
 
-        def cx(g, b):
-            x_grp[g, b] = group_words("x_grp%d%d" % (g, b), x_tp[g, b])
+        def op_tx(eng, tag, g, b):
+            x_tp[g, b] = transpose_words("x_tp%d%d" % (g, b), [x_raw[g, 2 * b], x_raw[g, 2 * b + 1]], tag)
 
-        def qx(g, b):
+        def op_cx(eng, tag, g, b):
+            x_grp[g, b] = group_words(eng, "x_grp%d%d" % (g, b), x_tp[g, b])
+
+        def op_qx(eng, tag, g, b):
             x_cod[g, b], x_scl[g, b] = quantize("x%d%d" % (g, b), x_grp[g, b][:].rearrange("p s m j -> p (s m j)"), 256)
 
-        def wi(h):
+        def op_wi(eng, tag, h):
             w_grp[h] = sb.tile([P, P, 4], BF16, name="w_grp%d" % h, align_bytes=64)
-            copy = nc.scalar.copy if h == 1 else nc.vector.tensor_copy
-            copy(out=w_grp[h][:], in_=w_raw[h // 2][:, h % 2].rearrange("p j c -> p c j"))
+            src = w_raw[h // 2][:, h % 2].rearrange("p j c -> p c j")
+            if eng == "G":
+                nc.gpsimd.tensor_scalar(out=w_grp[h][:], in0=src, scalar1=1.0, scalar2=0.0, op0=ALU.mult, op1=ALU.add)
+            else:
+                copier(eng)(out=w_grp[h][:], in_=src)
 
-        def qw(h):
+        def op_qw(eng, tag, h):
             w_cod[h], w_scl[h] = quantize("w%d" % h, w_grp[h][:].rearrange("p c j -> p (c j)"), P)
 
-        def ta(i):
-            a_tp[i] = transpose_words("a_tp%d" % i, [a_raw[i][:, 0, :], a_raw[i][:, 1, :]])
+        def op_di(eng, tag, i):
+            a_srt[i] = sb.tile([P, 2, 2, P], F32, name="a_srt%d" % i)
+            copier(eng)(out=a_srt[i][:], in_=a_raw[i][:].bitcast(F32).rearrange("p g (r u) -> p g u r", u=2))
 
-        def ca(i):
-            a_grp[i] = group_words("a_grp%d" % i, a_tp[i], on_vector=(i == 0))
+        def op_ta(eng, tag, i):
+            if i in SORTED_FIRST:
+                a_tp[i] = bank([P, 4, P], F32, "a_tp%d" % i, tag)
+                for s in range(2):
+                    for u in range(2):
+                        nc.tensor.transpose(a_tp[i][:, 2 * s + u, :], a_srt[i][:, s, u, :], ident[:])
+            else:
+                a_tp[i] = transpose_words("a_tp%d" % i, [a_raw[i][:, 0, :], a_raw[i][:, 1, :]], tag)
 
-        def qa(i):
+        def op_ca(eng, tag, i):
+            a_grp[i] = group_words(eng, "a_grp%d" % i, a_tp[i])
+
+        def op_qa(eng, tag, i):
             a_cod[i], a_scl[i] = quantize("a%d" % i, a_grp[i][:].rearrange("p g r j -> p (g r j)"), 256)
 
-        for g in range(2):
-            g_cod[g] = sb.tile([P, 512], U32, name="g_cod%d" % g, align_bytes=64)
-            g_scl[g] = sb.tile([P, 512], U8, name="g_scl%d" % g, align_bytes=64)
-
-        def s1(g, h):
-            g_ps[g, h] = ps.tile([P, 4, P], G_BANK_DT, name="g_ps%d%d" % (g, h), tag="acc", bufs=ACC_BANKS)
+        def op_s1(eng, tag, g, h):
+            g_ps[g, h] = bank([P, 4, P], BF16, "g_ps%d%d" % (g, h), tag)
             for t in range(4):
                 cols = slice(P * (t % 2), P * (t % 2 + 1))
                 nc.tensor.matmul_mx(out=g_ps[g, h][:, t, :],
@@ -130,19 +214,18 @@ def tile_gat_pa_kernel(tc, x, adj, W0, out):
                                     rhs=w_cod[h][:].bitcast(FP8X4), rhs_scale=w_scl[h][:],
                                     start=True, stop=True)
 
-        def cg(g, h):
+        def op_cg(eng, tag, g, h):
             g_grp[g, h] = sb.tile([P, P, 4], BF16, name="g_grp%d%d" % (g, h), align_bytes=64)
-            copy = nc.scalar.copy if h < 3 else nc.vector.tensor_copy
-            copy(out=g_grp[g, h][:], in_=g_ps[g, h][:].rearrange("p t c -> p c t"))
+            copier(eng)(out=g_grp[g, h][:], in_=g_ps[g, h][:].rearrange("p t c -> p c t"))
 
-        def qg(g, h):
+        def op_qg(eng, tag, g, h):
             cols = slice(P * h, P * (h + 1))
             nc.vector.quantize_mx(out=g_cod[g][:, cols].bitcast(FP8X4), scales=g_scl[g][:, cols],
                                   in_=g_grp[g, h][:].rearrange("p c t -> p (c t)"))
 
-        def s2(piece):
-            i, c0, width = piece
-            p_ps[piece] = ps.tile([P, width], F32, name="p_ps%d_%d" % (i, c0), tag="acc", bufs=ACC_BANKS)
+        def op_s2(eng, tag, i, c0, width):
+            piece = (i, c0, width)
+            p_ps[piece] = bank([P, width], F32, "p_ps%d_%d" % (i, c0), tag)
             for g in range(2):
                 rows = slice(P * g, P * (g + 1))
                 cols = slice(c0, c0 + width)
@@ -151,98 +234,89 @@ def tile_gat_pa_kernel(tc, x, adj, W0, out):
                                     rhs=g_cod[g][:, cols].bitcast(FP8X4), rhs_scale=g_scl[g][:, cols],
                                     start=(g == 0), stop=(g == 1))
 
-        def ee(piece):
-            e_sb[piece] = sb.tile([P, piece[2]], F32, name="e_sb%d_%d" % piece[0:2])
+        def op_ee(eng, tag, i, c0, width):
+            piece = (i, c0, width)
+            e_sb[piece] = sb.tile([P, width], F32, name="e_sb%d_%d" % (i, c0))
             nc.scalar.activation(out=e_sb[piece][:], in_=p_ps[piece][:], func=ACTF.Exp)
 
-        def mm(piece):
-            q_sb[piece] = sb.tile([P, piece[2]], F32, name="q_sb%d_%d" % piece[0:2])
-            if piece[0] == 6:
-                nc.scalar.activation(out=q_sb[piece][:], in_=e_sb[piece][:], func=ACTF.Relu, scale=-1.0, bias=1.0)
+        def op_mm(eng, tag, i, c0, width):
+            piece = (i, c0, width)
+            q_sb[piece] = sb.tile([P, width], F32, name="q_sb%d_%d" % (i, c0))
+            if eng == "S":
+                nc.scalar.activation(out=q_sb[piece][:], in_=e_sb[piece][:], func=ACTF.Copy, scale=1.0, bias=-1.0)
+            elif eng == "G":
+                nc.gpsimd.tensor_scalar(out=q_sb[piece][:], in0=e_sb[piece][:], scalar1=1.0, scalar2=-1.0,
+                                        op0=ALU.mult, op1=ALU.add)
             else:
-                nc.vector.tensor_scalar(out=q_sb[piece][:], in0=e_sb[piece][:], scalar1=-1.0, scalar2=0.0,
-                                        op0=ALU.add, op1=ALU.min)
+                nc.vector.tensor_scalar(out=q_sb[piece][:], in0=e_sb[piece][:], scalar1=1.0, scalar2=-1.0,
+                                        op0=ALU.mult, op1=ALU.add)
 
-        def ff(piece):
-            i, c0, width = piece
+        def op_ff(eng, tag, i, c0, width):
+            piece = (i, c0, width)
             o_sb = sb.tile([P, width], F32, name="o_sb%d_%d" % (i, c0))
             nc.vector.scalar_tensor_tensor(out=o_sb[:], in0=p_ps[piece][:], scalar=0.0, in1=q_sb[piece][:],
-                                           op0=ALU.max, op1=(ALU.subtract if i == 6 else ALU.add))
+                                           op0=ALU.max, op1=ALU.min)
             nc.sync.dma_start(out=out[P * i:P * (i + 1), c0:c0 + width], in_=o_sb[:])
 
-        keep_clock(4)
-        tx(0, 0)
-        tx(0, 1)
-        keep_clock(2)
-        tx(1, 0)
-        cx(0, 0)
-        tx(1, 1)
-        cx(0, 1)
-        wi(1)
-        cx(1, 0)
-        cx(1, 1)
-        qx(0, 0)
-        wi(0)
-        qx(0, 1)
-        qw(0)
-        qw(1)
-        wi(2)
-        wi(3)
-        qw(2)
-        qw(3)
-        qx(1, 0)
-        qx(1, 1)
+        ops = {"d": op_d, "tx": op_tx, "cx": op_cx, "qx": op_qx, "wi": op_wi, "qw": op_qw, "di": op_di, "ta": op_ta, "ca": op_ca,
+               "qa": op_qa, "s1": op_s1, "cg": op_cg, "qg": op_qg, "s2": op_s2, "ee": op_ee, "mm": op_mm, "ff": op_ff}
 
-        for g in range(2):
-            s1(g, 0)
-            s1(g, 1)
-            ta(g)
-            s1(g, 2)
-            s1(g, 3)
-            if g == 0:
-                ca(0)
-            cg(g, 0)
-            cg(g, 1)
-            cg(g, 2)
-            if g == 1:
-                ca(1)
-            qg(g, 0)
-            qg(g, 1)
-            cg(g, 3)
-            qg(g, 2)
-            qg(g, 3)
-            qa(g)
+        def needs(t):
+            k, a = t[0], tuple(t[1:])
+            if k == "cx":
+                return [("tx",) + a]
+            if k == "qx":
+                return [("cx",) + a]
+            if k == "qw":
+                return [("wi",) + a]
+            if k == "ta" and a[0] in SORTED_FIRST:
+                return [("di",) + a]
+            if k == "ca":
+                return [("ta",) + a]
+            if k == "qa":
+                return [("ca",) + a]
+            if k == "s1":
+                return [("qx", a[0], 0), ("qx", a[0], 1), ("qw", a[1])]
+            if k == "cg":
+                return [("s1",) + a]
+            if k == "qg":
+                return [("cg",) + a]
+            if k == "s2":
+                return [("qa", a[0])] + [("qg", g, h) for g in range(2) for h in range(4)]
+            if k == "ee":
+                return [("s2",) + a]
+            if k == "mm":
+                return [("ee",) + a]
+            if k == "ff":
+                return [("mm",) + a]
+            return []
 
-        whole = [(i, 0, 512) for i in range(7)]
-        halves = [(7, 0, 256), (7, 256, 256)]
-        for j in range(3):
-            now = whole[2 * j:2 * j + 2]
-            ahead = [2 * j + 2, 2 * j + 3]
-            for i in ahead:
-                ta(i)
-            for piece in now:
-                s2(piece)
-            for i in ahead:
-                ca(i)
-            for piece in now:
-                ee(piece)
-            if j > 0:
-                ff(whole[2 * j - 2])
-            for i in ahead:
-                qa(i)
-            if j > 0:
-                ff(whole[2 * j - 1])
-            for piece in now:
-                mm(piece)
-        for piece in [whole[6]] + halves:
-            s2(piece)
-        ee(whole[6])
-        mm(whole[6])
-        for piece in halves:
-            ee(piece)
-        for piece in whole[4:7]:
-            ff(piece)
-        for piece in halves:
-            mm(piece)
-        for piece in halves:
-            ff(piece)
+        reads_bank = {"cx": "tx", "ca": "ta", "cg": "s1", "ee": "s2", "ff": "s2"}
+
+        qs = queues()
+        done = set()
+        held = {"tp": [], "acc": []}
+        left = {}
+        pos = {"PE": 0, "S": 0, "V": 0, "G": 0}
+        total = sum([len(qs[e]) for e in qs])
+        while len(done) < total:
+            moved = False
+            for e in ("PE", "S", "V", "G"):
+                while pos[e] < len(qs[e]):
+                    entry = qs[e][pos[e]]
+                    t, tag = entry[0], entry[1]
+                    if not all([n in done for n in needs(t)]):
+                        break
+                    if tag is not None:
+                        h = held[tag]
+                        if len(h) >= BANKS[tag] and left[h[len(h) - BANKS[tag]]] > 0:
+                            break
+                        h.append(t)
+                        left[t] = READERS.get(t[0], 0)
+                    if t[0] in reads_bank:
+                        left[(reads_bank[t[0]],) + tuple(t[1:])] -= 1
+                    ops[t[0]](e, tag, *t[1:])
+                    done.add(t)
+                    pos[e] += 1
+                    moved = True
+            assert moved, "the queues cannot be merged"

@@ -16,7 +16,7 @@ ACTF = mybir.ActivationFunctionType
 P = 128
 BANKS = {"tp": 3, "acc": 5}
 READERS = {"tx": 1, "ta": 1, "s1": 1, "s2": 2}
-SORTED_FIRST = (4, 5, 6, 7)
+SORTED_FIRST = (4, 5)
 
 
 def queues():
@@ -68,8 +68,6 @@ def queues():
         if j == 0:
             v += plain("di", [(4,), (5,)])
         v += plain("qa", ahead)
-        if j == 0:
-            v += plain("di", [(6,), (7,)])
         if j > 0:
             v += each("ff", (2 * j - 1,))
         affine(now)

@@ -175,11 +175,8 @@ def tile_gat_pa_kernel(tc, x, adj, W0, out):
 
         def op_wi(eng, tag, h):
             w_grp[h] = sb.tile([P, P, 4], BF16, name="w_grp%d" % h, align_bytes=64)
-            src = w_raw[h // 2][:, h % 2].rearrange("p j c -> p c j")
-            if eng == "G":
-                nc.gpsimd.tensor_scalar(out=w_grp[h][:], in0=src, scalar1=1.0, scalar2=0.0, op0=ALU.mult, op1=ALU.add)
-            else:
-                copier(eng)(out=w_grp[h][:], in_=src)
+            copier(eng)(out=w_grp[h][:].rearrange("p (c i) j -> p c j i", i=4),
+                        in_=w_raw[h // 2][:, h % 2].rearrange("p j (c i) -> p c j i", i=4))
 
         def op_qw(eng, tag, h):
             w_cod[h], w_scl[h] = quantize("w%d" % h, w_grp[h][:].rearrange("p c j -> p (c j)"), P)

@@ -16,6 +16,7 @@ ACTF = mybir.ActivationFunctionType
 P = 128
 BANKS = {"tp": 3, "acc": 5}
 READERS = {"tx": 1, "ta": 1, "s1": 1, "s2": 2}
+COPIED_BY_VECTOR = (5,)
 SORTED_FIRST = (4, 5)
 
 
@@ -23,8 +24,6 @@ def queues():
     whole = [(i, 0, 512) for i in range(7)]
     halves = [(7, 0, 256), (7, 256, 256)]
     pieces = whole + halves
-    on_gpsimd = ()
-    on_scalar = (6,)
 
     def each(op, strips):
         return [((op,) + p, None) for p in pieces if p[0] in strips]
@@ -49,35 +48,22 @@ def queues():
             s += plain("ca", [(1,)])
         v += plain("qg", [(h, 0), (h, 1)]) + plain("cg", [(h, 3)]) + plain("qg", [(h, 2), (h, 3)]) + plain("qa", [(h,)])
 
-    def affine(strips):
-        for i in strips:
-            if i in on_gpsimd:
-                g.extend(each("mm", (i,)))
-            elif i in on_scalar:
-                s.extend(each("mm", (i,)))
-            else:
-                v.extend(each("mm", (i,)))
-
     for j in range(3):
         now = (2 * j, 2 * j + 1)
-        ahead = [(2 * j + 2,), (2 * j + 3,)]
-        pe += opens("ta", ahead, "tp") + opens("s2", [p for p in pieces if p[0] in now], "acc")
-        s += plain("ca", ahead) + each("ee", now)
-        if j > 0:
-            v += each("ff", (2 * j - 2,))
+        a, b = 2 * j + 2, 2 * j + 3
+        pe += opens("ta", [(a,), (b,)], "tp") + opens("s2", [p for p in pieces if p[0] in now], "acc")
+        by_vector = [(i,) for i in (a, b) if i in COPIED_BY_VECTOR]
+        s += plain("ca", [(i,) for i in (a, b) if i not in COPIED_BY_VECTOR]) + each("ee", now)
+        g += each("mm", now)
         if j == 0:
             v += plain("di", [(4,), (5,)])
-        v += plain("qa", ahead)
+        v += plain("ca", by_vector) + plain("qa", [(a,), (b,)])
         if j > 0:
-            v += each("ff", (2 * j - 1,))
-        affine(now)
+            v += each("ff", (2 * j - 2, 2 * j - 1))
     pe += opens("s2", [p for p in pieces if p[0] in (6, 7)], "acc")
-    s += each("ee", (6,))
-    affine((6,))
-    s += each("ee", (7,))
-    v += each("ff", (4, 5, 6))
-    affine((7,))
-    v += each("ff", (7,))
+    s += each("ee", (6, 7))
+    g += each("mm", (6, 7))
+    v += each("ff", (4, 5, 6, 7))
     return {"PE": pe, "S": s, "V": v, "G": g}
 
 

@@ -16,7 +16,6 @@ ACTF = mybir.ActivationFunctionType
 P = 128
 BANKS = {"tp": 3, "acc": 5}
 READERS = {"tx": 1, "ta": 1, "s1": 1, "s2": 2}
-COPIED_BY_VECTOR = (5,)
 SORTED_FIRST = (4, 5)
 
 
@@ -24,6 +23,8 @@ def queues():
     whole = [(i, 0, 512) for i in range(7)]
     halves = [(7, 0, 256), (7, 256, 256)]
     pieces = whole + halves
+    on_gpsimd = ()
+    on_scalar = (6,)
 
     def each(op, strips):
         return [((op,) + p, None) for p in pieces if p[0] in strips]
@@ -35,35 +36,20 @@ def queues():
         return [((op,) + tuple(a), tag) for a in args]
 
     pe = [(("d", 4, 0), "acc")] + opens("tx", [(0, 0), (0, 1)], "tp") + [(("d", 2, 1), None)] + opens("tx", [(1, 0), (1, 1)], "tp")
-    s = plain("cx", [(0, 0), (0, 1)]) + plain("wi", [(1,)]) + plain("cx", [(1, 0), (1, 1)])
-    v = plain("qx", [(0, 0)]) + plain("wi", [(0,)]) + plain("qx", [(0, 1)]) + plain("qw", [(0,), (1,)])
-    v += plain("wi", [(2,), (3,)]) + plain("qw", [(2,), (3,)]) + plain("qx", [(1, 0), (1, 1)])
-    g = []
-    for h in range(2):
-        pe += opens("s1", [(h, 0), (h, 1)], "acc") + opens("ta", [(h,)], "tp") + opens("s1", [(h, 2), (h, 3)], "acc")
-        s += plain("cg", [(h, 0), (h, 1), (h, 2)])
-        if h == 0:
-            v += plain("ca", [(0,)])
-        else:
-            s += plain("ca", [(1,)])
-        v += plain("qg", [(h, 0), (h, 1)]) + plain("cg", [(h, 3)]) + plain("qg", [(h, 2), (h, 3)]) + plain("qa", [(h,)])
-
-    for j in range(3):
-        now = (2 * j, 2 * j + 1)
-        a, b = 2 * j + 2, 2 * j + 3
-        pe += opens("ta", [(a,), (b,)], "tp") + opens("s2", [p for p in pieces if p[0] in now], "acc")
-        by_vector = [(i,) for i in (a, b) if i in COPIED_BY_VECTOR]
-        s += plain("ca", [(i,) for i in (a, b) if i not in COPIED_BY_VECTOR]) + each("ee", now)
-        g += each("mm", now)
-        if j == 0:
-            v += plain("di", [(4,), (5,)])
-        v += plain("ca", by_vector) + plain("qa", [(a,), (b,)])
-        if j > 0:
-            v += each("ff", (2 * j - 2, 2 * j - 1))
-    pe += opens("s2", [p for p in pieces if p[0] in (6, 7)], "acc")
-    s += each("ee", (6, 7))
-    g += each("mm", (6, 7))
-    v += each("ff", (4, 5, 6, 7))
+    pe += opens("s1", [(0, 0)], "acc") + opens("ta", [(0,)], "tp") + opens("s1", [(0, 1), (0, 2), (0, 3), (1, 0), (1, 1), (1, 2), (1, 3)], "acc")
+    pe += opens("ta", [(1,), (2,), (3,)], "tp") + opens("s2", [p for p in pieces if p[0] in (0, 1)], "acc")
+    pe += opens("ta", [(4,), (5,)], "tp") + opens("s2", [p for p in pieces if p[0] in (2, 3)], "acc")
+    pe += opens("ta", [(6,), (7,)], "tp") + opens("s2", [p for p in pieces if p[0] in (4, 5, 6, 7)], "acc")
+    s = plain("cx", [(0, 1)]) + plain("wi", [(1,)]) + plain("cx", [(1, 0), (1, 1)])
+    s += plain("cg", [(0, 0)]) + plain("cg", [(0, 1), (0, 2), (1, 0), (1, 1), (1, 2)])
+    s += plain("ca", [(1,), (2,), (3,)]) + each("ee", (0, 1)) + plain("ca", [(4,)]) + each("ee", (2, 3)) + plain("ca", [(6,), (7,)]) + each("ee", (4, 5, 6))
+    s += [(("ee", 7, 0, 256), None), (("mm", 6, 0, 512), None), (("ee", 7, 256, 256), None)] + each("mm", (7,))
+    v = plain("cx", [(0, 0)]) + plain("qx", [(0, 0)]) + plain("wi", [(0,)]) + plain("qx", [(0, 1)]) + plain("qw", [(0,)]) + plain("wi", [(2,), (3,)]) + plain("qw", [(1,), (2,), (3,)])
+    v += plain("qx", [(1, 0), (1, 1)])
+    v += plain("ca", [(0,)]) + plain("qg", [(0, 0)]) + plain("qa", [(0,)]) + plain("cg", [(0, 3)]) + plain("qg", [(0, 1), (0, 2)]) + plain("cg", [(1, 3)]) + plain("qg", [(0, 3), (1, 0), (1, 1), (1, 2), (1, 3)])
+    v += plain("qa", [(1,)]) + plain("di", [(4,), (5,)]) + plain("qa", [(2,), (3,)]) + plain("ca", [(5,)]) + each("ff", (0,)) + plain("qa", [(4,), (5,)]) + each("ff", (1, 2))
+    v += plain("qa", [(6,), (7,)]) + each("ff", (3, 4, 5, 6, 7))
+    g = each("mm", (0, 1, 2, 3, 4, 5))
     return {"PE": pe, "S": s, "V": v, "G": g}
 
 

@@ -36,18 +36,18 @@ def queues():
         return [((op,) + tuple(a), tag) for a in args]
 
     pe = [(("d", 4, 0), "acc")] + opens("tx", [(0, 0), (0, 1)], "tp") + [(("d", 2, 1), None)] + opens("tx", [(1, 0), (1, 1)], "tp")
-    pe += opens("s1", [(0, 0)], "acc") + opens("ta", [(0,)], "tp") + opens("s1", [(0, 1), (0, 2), (0, 3), (1, 0), (1, 1), (1, 2), (1, 3)], "acc")
-    pe += opens("ta", [(1,), (2,), (3,)], "tp") + opens("s2", [p for p in pieces if p[0] in (0, 1)], "acc")
+    pe += opens("s1", [(0, 0), (0, 1)], "acc") + opens("ta", [(0,), (1,)], "tp") + opens("s1", [(0, 2), (0, 3), (1, 0), (1, 1), (1, 2), (1, 3)], "acc")
+    pe += opens("ta", [(2,), (3,)], "tp") + opens("s2", [p for p in pieces if p[0] in (0, 1)], "acc")
     pe += opens("ta", [(4,), (5,)], "tp") + opens("s2", [p for p in pieces if p[0] in (2, 3)], "acc")
     pe += opens("ta", [(6,), (7,)], "tp") + opens("s2", [p for p in pieces if p[0] in (4, 5, 6, 7)], "acc")
     s = plain("cx", [(0, 1)]) + plain("wi", [(1,)]) + plain("cx", [(1, 0), (1, 1)])
-    s += plain("cg", [(0, 0)]) + plain("cg", [(0, 1), (0, 2), (1, 0), (1, 1), (1, 2)])
-    s += plain("ca", [(1,), (2,), (3,)]) + each("ee", (0, 1)) + plain("ca", [(4,)]) + each("ee", (2, 3)) + plain("ca", [(6,), (7,)]) + each("ee", (4, 5, 6))
+    s += plain("cg", [(0, 0), (0, 1), (0, 2), (1, 0), (1, 1), (1, 2)]) + plain("ca", [(1,)])
+    s += plain("ca", [(2,), (3,)]) + each("ee", (0, 1)) + plain("ca", [(4,)]) + each("ee", (2, 3)) + plain("ca", [(6,), (7,)]) + each("ee", (4, 5, 6))
     s += [(("ee", 7, 0, 256), None), (("mm", 6, 0, 512), None), (("ee", 7, 256, 256), None)] + each("mm", (7,))
-    v = plain("cx", [(0, 0)]) + plain("qx", [(0, 0)]) + plain("wi", [(0,)]) + plain("qx", [(0, 1)]) + plain("qw", [(0,)]) + plain("wi", [(2,), (3,)]) + plain("qw", [(1,), (2,), (3,)])
+    v = plain("cx", [(0, 0)]) + plain("qx", [(0, 0)]) + plain("wi", [(0,)]) + plain("qx", [(0, 1)]) + plain("qw", [(0,), (1,)]) + plain("wi", [(2,), (3,)]) + plain("qw", [(2,), (3,)])
     v += plain("qx", [(1, 0), (1, 1)])
-    v += plain("ca", [(0,)]) + plain("qg", [(0, 0)]) + plain("qa", [(0,)]) + plain("cg", [(0, 3)]) + plain("qg", [(0, 1), (0, 2)]) + plain("cg", [(1, 3)]) + plain("qg", [(0, 3), (1, 0), (1, 1), (1, 2), (1, 3)])
-    v += plain("qa", [(1,)]) + plain("di", [(4,), (5,)]) + plain("qa", [(2,), (3,)]) + plain("ca", [(5,)]) + each("ff", (0,)) + plain("qa", [(4,), (5,)]) + each("ff", (1, 2))
+    v += plain("ca", [(0,)]) + plain("qg", [(0, 0)]) + plain("qa", [(0,)]) + plain("cg", [(0, 3)]) + plain("qg", [(0, 1), (0, 2)]) + plain("cg", [(1, 3)]) + plain("qg", [(0, 3), (1, 0), (1, 1), (1, 2), (1, 3)]) + plain("qa", [(1,)])
+    v += plain("di", [(4,), (5,)]) + plain("qa", [(2,), (3,)]) + plain("ca", [(5,)]) + each("ff", (0,)) + plain("qa", [(4,), (5,)]) + each("ff", (1, 2))
     v += plain("qa", [(6,), (7,)]) + each("ff", (3, 4, 5, 6, 7))
     g = each("mm", (0, 1, 2, 3, 4, 5))
     return {"PE": pe, "S": s, "V": v, "G": g}

from contextlib import ExitStack

import concourse.mybir as mybir
from concourse.masks import make_identity

FLOPS = 2 * 1024 * 512 * 512 + 2 * 1024 * 1024 * 512

F32 = mybir.dt.float32
BF16 = mybir.dt.bfloat16
U32 = mybir.dt.uint32
U8 = mybir.dt.uint8
FP8X4 = mybir.dt.float8_e4m3fn_x4
ALU = mybir.AluOpType
ACTF = mybir.ActivationFunctionType

P = 128
BANKS = {"tp": 3, "acc": 5}
READERS = {"tx": 1, "ta": 1, "s1": 1, "s2": 2}
SORTED_FIRST = (4, 5)


def queues():
    whole = [(i, 0, 512) for i in range(7)]
    halves = [(7, 0, 256), (7, 256, 256)]
    pieces = whole + halves
    on_gpsimd = ()
    on_scalar = (6,)

    def each(op, strips):
        return [((op,) + p, None) for p in pieces if p[0] in strips]

    def plain(op, args):
        return [((op,) + tuple(a), None) for a in args]

    def opens(op, args, tag):
        return [((op,) + tuple(a), tag) for a in args]

    pe = [(("d", 4, 0), "acc")] + opens("tx", [(0, 0), (0, 1)], "tp") + [(("d", 2, 1), None)] + opens("tx", [(1, 0), (1, 1)], "tp")
    pe += opens("s1", [(0, 0), (0, 1)], "acc") + opens("ta", [(0,), (1,)], "tp") + opens("s1", [(0, 2), (0, 3), (1, 0), (1, 1), (1, 2), (1, 3)], "acc")
    pe += opens("ta", [(2,), (3,)], "tp") + opens("s2", [p for p in pieces if p[0] in (0, 1)], "acc")
    pe += opens("ta", [(4,), (5,)], "tp") + opens("s2", [p for p in pieces if p[0] in (2, 3)], "acc")
    pe += opens("ta", [(6,), (7,)], "tp") + opens("s2", [p for p in pieces if p[0] in (4, 5, 6, 7)], "acc")
    s = plain("cx", [(0, 1)]) + plain("wi", [(1,)]) + plain("cx", [(1, 0), (1, 1)])
    s += plain("cg", [(0, 0), (0, 1), (0, 2), (1, 0), (1, 1), (1, 2)]) + plain("ca", [(1,)])
    s += plain("ca", [(2,), (3,)]) + each("ee", (0, 1)) + plain("ca", [(4,)]) + each("ee", (2, 3)) + plain("ca", [(6,), (7,)]) + each("ee", (4, 5, 6))
    s += [(("ee", 7, 0, 256), None), (("mm", 6, 0, 512), None), (("ee", 7, 256, 256), None)] + each("mm", (7,))
    v = plain("cx", [(0, 0)]) + plain("qx", [(0, 0)]) + plain("wi", [(0,)]) + plain("qx", [(0, 1)]) + plain("qw", [(0,), (1,)]) + plain("wi", [(2,), (3,)]) + plain("qw", [(2,), (3,)])
    v += plain("qx", [(1, 0), (1, 1)])
    v += plain("ca", [(0,)]) + plain("qg", [(0, 0)]) + plain("qa", [(0,)]) + plain("cg", [(0, 3)]) + plain("qg", [(0, 1), (0, 2)]) + plain("cg", [(1, 3)]) + plain("qg", [(0, 3), (1, 0), (1, 1), (1, 2), (1, 3)]) + plain("qa", [(1,)])
    v += plain("di", [(4,), (5,)]) + plain("qa", [(2,), (3,)]) + plain("ca", [(5,)]) + each("ff", (0,)) + plain("qa", [(4,), (5,)]) + each("ff", (1, 2))
    v += plain("qa", [(6,), (7,)]) + each("ff", (3, 4, 5, 6, 7))
    g = each("mm", (0, 1, 2, 3, 4, 5))
    return {"PE": pe, "S": s, "V": v, "G": g}


def tile_gat_pa_kernel(tc, x, adj, W0, out):
    nc = tc.nc
    with ExitStack() as ctx:
        sb = ctx.enter_context(tc.tile_pool(name="sb", bufs=1))
        ps = ctx.enter_context(tc.psum_pool(name="ps", bufs=1))
        ctx.enter_context(tc.manual_schedule())

        x_raw, x_tp, x_grp, x_cod, x_scl = {}, {}, {}, {}, {}
        w_raw, w_grp, w_cod, w_scl = {}, {}, {}, {}
        a_raw, a_tp, a_grp, a_cod, a_scl = {}, {}, {}, {}, {}
        a_srt = {}
        g_ps, g_grp, g_cod, g_scl = {}, {}, {}, {}
        p_ps, e_sb, q_sb = {}, {}, {}
        idle = {}

        def load_x(g, t0, n):
            raw = sb.tile([P, n, 512], BF16, name="x_raw%d%d" % (g, t0))
            rows = x[512 * g:512 * (g + 1), :].rearrange("(m t) k -> m t k", t=4)
            nc.sync.dma_start(out=raw[:], in_=rows[:, t0:t0 + n, :])
            for s in range(n):
                x_raw[g, t0 + s] = raw[:, s, :]

        def load_w(a):
            w_raw[a] = sb.tile([P, 2, 4, P], BF16, name="w_raw%d" % a)
            nc.sync.dma_start(out=w_raw[a][:], in_=W0[2 * a:2 * a + 2].rearrange("h (p j) c -> p h j c", j=4))

        def load_adj(i):
            a_raw[i] = sb.tile([P, 2, 512], BF16, name="a_raw%d" % i)
            nc.sync.dma_start(out=a_raw[i][:], in_=adj[P * i:P * (i + 1), :].rearrange("n (g m) -> n g m", g=2))

        load_x(0, 0, 2)
        load_x(0, 2, 2)
        load_x(1, 0, 2)
        load_w(0)
        load_x(1, 2, 1)
        load_x(1, 3, 1)
        load_w(1)
        for i in range(8):
            load_adj(i)

        zeros = sb.tile([P, 512], BF16, name="zeros")
        nc.vector.memset(zeros[:], 0.0)
        exp_in = sb.tile([P, 1], F32, name="exp_in")
        exp_out = sb.tile([P, 1], F32, name="exp_out")
        nc.vector.memset(exp_in[:], 0.0)
        nc.scalar.activation(out=exp_out[:], in_=exp_in[:], func=ACTF.Exp)
        ident = sb.tile([P, P], F32, name="ident")
        make_identity(nc, ident[:])
        for g in range(2):
            g_cod[g] = sb.tile([P, 512], U32, name="g_cod%d" % g, align_bytes=64)
            g_scl[g] = sb.tile([P, 512], U8, name="g_scl%d" % g, align_bytes=64)

        def copier(eng):
            return nc.vector.tensor_copy if eng == "V" else nc.scalar.copy

        def bank(shape, dt, name, tag):
            return ps.tile(shape, dt, name=name, tag=tag, bufs=BANKS[tag])

        def transpose_words(name, rows512, tag):
            t = bank([P, 4, P], F32, name, tag)
            for s in range(2):
                words = rows512[s].bitcast(F32)
                for u in range(2):
                    nc.tensor.transpose(t[:, 2 * s + u, :], words[:, u:256:2], ident[:])
            return t

        def group_words(eng, name, t):
            grp = sb.tile([P, 2, P, 4], BF16, name=name, align_bytes=64)
            copier(eng)(out=grp[:].bitcast(F32), in_=t[:].rearrange("p (s u) r -> p s r u", u=2))
            return grp

        def quantize(name, grp2d, width):
            cod = sb.tile([P, width], U32, name=name + "_cod", align_bytes=64)
            scl = sb.tile([P, width], U8, name=name + "_scl", align_bytes=64)
            nc.vector.quantize_mx(out=cod[:].bitcast(FP8X4), scales=scl[:], in_=grp2d)
            return cod, scl

        def op_d(eng, tag, n, k):
            if tag is not None:
                idle["ps"] = bank([P, 512], F32, "idle_ps", tag)
            for r in range(n):
                nc.tensor.matmul(out=idle["ps"][:], lhsT=zeros[:, 0:P], rhs=zeros[:], start=True, stop=True)

        def op_tx(eng, tag, g, b):
            x_tp[g, b] = transpose_words("x_tp%d%d" % (g, b), [x_raw[g, 2 * b], x_raw[g, 2 * b + 1]], tag)

        def op_cx(eng, tag, g, b):
            x_grp[g, b] = group_words(eng, "x_grp%d%d" % (g, b), x_tp[g, b])

        def op_qx(eng, tag, g, b):
            x_cod[g, b], x_scl[g, b] = quantize("x%d%d" % (g, b), x_grp[g, b][:].rearrange("p s m j -> p (s m j)"), 256)

        def op_wi(eng, tag, h):
            w_grp[h] = sb.tile([P, P, 4], BF16, name="w_grp%d" % h, align_bytes=64)
            copier(eng)(out=w_grp[h][:].rearrange("p (c i) j -> p c j i", i=4),
                        in_=w_raw[h // 2][:, h % 2].rearrange("p j (c i) -> p c j i", i=4))

        def op_qw(eng, tag, h):
            w_cod[h], w_scl[h] = quantize("w%d" % h, w_grp[h][:].rearrange("p c j -> p (c j)"), P)

        def op_di(eng, tag, i):
            a_srt[i] = sb.tile([P, 2, 2, P], F32, name="a_srt%d" % i)
            copier(eng)(out=a_srt[i][:], in_=a_raw[i][:].bitcast(F32).rearrange("p g (r u) -> p g u r", u=2))

        def op_ta(eng, tag, i):
            if i in SORTED_FIRST:
                a_tp[i] = bank([P, 4, P], F32, "a_tp%d" % i, tag)
                for s in range(2):
                    for u in range(2):
                        nc.tensor.transpose(a_tp[i][:, 2 * s + u, :], a_srt[i][:, s, u, :], ident[:])
            else:
                a_tp[i] = transpose_words("a_tp%d" % i, [a_raw[i][:, 0, :], a_raw[i][:, 1, :]], tag)

        def op_ca(eng, tag, i):
            a_grp[i] = group_words(eng, "a_grp%d" % i, a_tp[i])

        def op_qa(eng, tag, i):
            a_cod[i], a_scl[i] = quantize("a%d" % i, a_grp[i][:].rearrange("p g r j -> p (g r j)"), 256)

        def op_s1(eng, tag, g, h):
            g_ps[g, h] = bank([P, 4, P], BF16, "g_ps%d%d" % (g, h), tag)
            for t in range(4):
                cols = slice(P * (t % 2), P * (t % 2 + 1))
                nc.tensor.matmul_mx(out=g_ps[g, h][:, t, :],
                                    lhsT=x_cod[g, t // 2][:, cols].bitcast(FP8X4), lhsT_scale=x_scl[g, t // 2][:, cols],
                                    rhs=w_cod[h][:].bitcast(FP8X4), rhs_scale=w_scl[h][:],
                                    start=True, stop=True)

        def op_cg(eng, tag, g, h):
            g_grp[g, h] = sb.tile([P, P, 4], BF16, name="g_grp%d%d" % (g, h), align_bytes=64)
            copier(eng)(out=g_grp[g, h][:], in_=g_ps[g, h][:].rearrange("p t c -> p c t"))

        def op_qg(eng, tag, g, h):
            cols = slice(P * h, P * (h + 1))
            nc.vector.quantize_mx(out=g_cod[g][:, cols].bitcast(FP8X4), scales=g_scl[g][:, cols],
                                  in_=g_grp[g, h][:].rearrange("p c t -> p (c t)"))

        def op_s2(eng, tag, i, c0, width):
            piece = (i, c0, width)
            p_ps[piece] = bank([P, width], F32, "p_ps%d_%d" % (i, c0), tag)
            for g in range(2):
                rows = slice(P * g, P * (g + 1))
                cols = slice(c0, c0 + width)
                nc.tensor.matmul_mx(out=p_ps[piece][:],
                                    lhsT=a_cod[i][:, rows].bitcast(FP8X4), lhsT_scale=a_scl[i][:, rows],
                                    rhs=g_cod[g][:, cols].bitcast(FP8X4), rhs_scale=g_scl[g][:, cols],
                                    start=(g == 0), stop=(g == 1))

        def op_ee(eng, tag, i, c0, width):
            piece = (i, c0, width)
            e_sb[piece] = sb.tile([P, width], F32, name="e_sb%d_%d" % (i, c0))
            nc.scalar.activation(out=e_sb[piece][:], in_=p_ps[piece][:], func=ACTF.Exp)

        def op_mm(eng, tag, i, c0, width):
            piece = (i, c0, width)
            q_sb[piece] = sb.tile([P, width], F32, name="q_sb%d_%d" % (i, c0))
            if eng == "S":
                nc.scalar.activation(out=q_sb[piece][:], in_=e_sb[piece][:], func=ACTF.Copy, scale=1.0, bias=-1.0)
            elif eng == "G":
                nc.gpsimd.tensor_scalar(out=q_sb[piece][:], in0=e_sb[piece][:], scalar1=1.0, scalar2=-1.0,
                                        op0=ALU.mult, op1=ALU.add)
            else:
                nc.vector.tensor_scalar(out=q_sb[piece][:], in0=e_sb[piece][:], scalar1=1.0, scalar2=-1.0,
                                        op0=ALU.mult, op1=ALU.add)

        def op_ff(eng, tag, i, c0, width):
            piece = (i, c0, width)
            o_sb = sb.tile([P, width], F32, name="o_sb%d_%d" % (i, c0))
            nc.vector.scalar_tensor_tensor(out=o_sb[:], in0=p_ps[piece][:], scalar=0.0, in1=q_sb[piece][:],
                                           op0=ALU.max, op1=ALU.min)
            nc.sync.dma_start(out=out[P * i:P * (i + 1), c0:c0 + width], in_=o_sb[:])

        ops = {"d": op_d, "tx": op_tx, "cx": op_cx, "qx": op_qx, "wi": op_wi, "qw": op_qw, "di": op_di, "ta": op_ta, "ca": op_ca,
               "qa": op_qa, "s1": op_s1, "cg": op_cg, "qg": op_qg, "s2": op_s2, "ee": op_ee, "mm": op_mm, "ff": op_ff}

        def needs(t):
            k, a = t[0], tuple(t[1:])
            if k == "cx":
                return [("tx",) + a]
            if k == "qx":
                return [("cx",) + a]
            if k == "qw":
                return [("wi",) + a]
            if k == "ta" and a[0] in SORTED_FIRST:
                return [("di",) + a]
            if k == "ca":
                return [("ta",) + a]
            if k == "qa":
                return [("ca",) + a]
            if k == "s1":
                return [("qx", a[0], 0), ("qx", a[0], 1), ("qw", a[1])]
            if k == "cg":
                return [("s1",) + a]
            if k == "qg":
                return [("cg",) + a]
            if k == "s2":
                return [("qa", a[0])] + [("qg", g, h) for g in range(2) for h in range(4)]
            if k == "ee":
                return [("s2",) + a]
            if k == "mm":
                return [("ee",) + a]
            if k == "ff":
                return [("mm",) + a]
            return []

        reads_bank = {"cx": "tx", "ca": "ta", "cg": "s1", "ee": "s2", "ff": "s2"}

        qs = queues()
        done = set()
        held = {"tp": [], "acc": []}
        left = {}
        pos = {"PE": 0, "S": 0, "V": 0, "G": 0}
        total = sum([len(qs[e]) for e in qs])
        while len(done) < total:
            moved = False
            for e in ("PE", "S", "V", "G"):
                while pos[e] < len(qs[e]):
                    entry = qs[e][pos[e]]
                    t, tag = entry[0], entry[1]
                    if not all([n in done for n in needs(t)]):
                        break
                    if tag is not None:
                        h = held[tag]
                        if len(h) >= BANKS[tag] and left[h[len(h) - BANKS[tag]]] > 0:
                            break
                        h.append(t)
                        left[t] = READERS.get(t[0], 0)
                    if t[0] in reads_bank:
                        left[(reads_bank[t[0]],) + tuple(t[1:])] -= 1
                    ops[t[0]](e, tag, *t[1:])
                    done.add(t)
                    pos[e] += 1
                    moved = True
            assert moved, "the queues cannot be merged"
